import numpy as np
import ml_dtypes


def mxq(x, axis, fmt="e4m3"):
    dtype, down = {"e4m3": (ml_dtypes.float8_e4m3fn, 7), "e5m2": (ml_dtypes.float8_e5m2, 14)}[fmt]
    v = np.moveaxis(np.asarray(x, np.float32).astype(ml_dtypes.bfloat16).astype(np.float64), axis, -1)
    blocks = v.reshape(v.shape[:-1] + (-1, 32))
    amax = np.abs(blocks).max(-1, keepdims=True)
    byte = np.maximum(np.where(amax > 0, np.frexp(amax)[1] - 1 + 127, 0) - down, 1)
    scale = np.exp2(byte - 127.0)
    codes = (blocks / scale).astype(np.float32).astype(dtype).astype(np.float64)
    return np.moveaxis((codes * scale).reshape(v.shape), -1, axis)


WIDE = False


def mx_kscale(k):
    if not WIDE:
        return np.ones(k)
    levels = np.array([10, -10, 5, -5, 0])
    a = np.random.permutation(np.resize(levels, k // 512 * 4)).reshape(k // 512, 4)
    idx = np.arange(k)
    return np.exp2(a[idx // 512, idx % 128 // 32])


BF16 = ml_dtypes.bfloat16


def bf(x):
    return np.asarray(x, np.float32).astype(BF16)


def f64(x):
    return np.asarray(x).astype(np.float64)


BS, CIN, H, D, L, P, OUT_DIM = 32, 256, 256, 1024, 10, 2, 128
K0, K1 = CIN * P, H * P


def patch_conv_relu(y, w):
    bs, cin, d = y.shape
    out, p = w.shape[0], w.shape[-1]
    q = d // p
    rows = y.reshape(bs, cin, q, p).transpose(0, 2, 1, 3).reshape(bs * q, cin * p)
    wm = w.reshape(out, cin * p).T
    z = (mxq(rows, 1, "e4m3") @ mxq(wm, 0, "e4m3")) * (1.0 / np.sqrt(cin))
    return np.maximum(z, 0.0).reshape(bs, q, out).transpose(0, 2, 1)


def setup_inputs():
    s = mx_kscale(K0).reshape(CIN, P)
    t = mx_kscale(K1)[::P]
    return {"x": bf(np.random.standard_normal((BS, CIN, D)) * np.tile(s, (1, D // P))),
            "w0": bf(np.random.standard_normal((H, CIN, P)) / s * t[:, None, None]),
            "w1": bf(np.random.standard_normal((H, H, P)) / t[:, None])}


def reference(x, w0, w1):
    h = patch_conv_relu(f64(x), f64(w0))
    return patch_conv_relu(h, f64(w1))

@@ -1,0 +1,153 @@
+from contextlib import ExitStack
+
+import concourse.mybir as mybir
+from concourse.masks import make_identity
+
+FP8X4 = mybir.dt.float8_e4m3fn_x4
+BF16 = mybir.dt.bfloat16
+F32 = mybir.dt.float32
+U32 = mybir.dt.uint32
+U8 = mybir.dt.uint8
+RELU = mybir.ActivationFunctionType.Relu
+MULT = mybir.AluOpType.mult
+MAX = mybir.AluOpType.max
+
+P = 128
+BS = 32
+D = 1024
+Q1 = 512
+Q2 = 256
+SCALE = 1.0 / 16.0
+
+FLOPS = 2 * BS * Q1 * 512 * 256 + 2 * BS * Q2 * 512 * 256
+
+CHUNKS = [1, 1, 1, 1] + [2] * 13 + [1, 1]
+RAW_BUFS = 10
+VECTOR_EXIT_EVERY = 5
+
+
+def tile_cnn_pa_kernel(tc, x, w0, w1, out):
+    nc = tc.nc
+    spans = []
+    first = 0
+    for nb in CHUNKS:
+        spans.append((first, nb))
+        first += nb
+    assert first == BS
+    n = len(spans)
+
+    with ExitStack() as ctx:
+        const = ctx.enter_context(tc.tile_pool(name="const", bufs=1))
+        raw_pool = ctx.enter_context(tc.tile_pool(name="rawp", bufs=RAW_BUFS))
+        work = ctx.enter_context(tc.tile_pool(name="work", bufs=3))
+        psum1 = ctx.enter_context(tc.psum_pool(name="psum1", bufs=4))
+        psum2 = ctx.enter_context(tc.psum_pool(name="psum2", bufs=4))
+
+        ident = const.tile([P, P], F32, name="ident")
+        make_identity(nc, ident[:])
+        out_all = const.tile([P, BS, 2 * Q2], F32, name="out_all")
+
+        raw = {}
+
+        def load(i):
+            b0, nb = spans[i]
+            t = raw_pool.tile([P, nb * 2 * D], BF16, name="raw%d" % i, tag="raw")
+            nc.sync.dma_start(
+                out=t[:].rearrange("p (b e) -> p b e", b=nb),
+                in_=x[b0 : b0 + nb].rearrange("b (p u) d -> p b (u d)", u=2),
+            )
+            raw[i] = t
+
+        def load_weight(w, label):
+            rows = const.tile([P, 1024], BF16, name=label + "_rows")
+            nc.sync.dma_start(out=rows[:], in_=w.rearrange("(p a) c k -> p (a c k)", a=2))
+            return rows
+
+        def prepare_weight(rows, label):
+            words = rows[:].bitcast(F32).rearrange("p (a c u) -> p a c u", a=2, u=2)
+            bank = psum2.tile([P, 2, 256], F32, name=label + "_bank", tag="ps2")
+            for u in range(2):
+                for a in range(2):
+                    nc.tensor.transpose(bank[:, u, a * P : (a + 1) * P], words[:, a, :, u], ident[:])
+            grouped = const.tile([P, 1024], BF16, name=label + "_grouped", align_bytes=64)
+            nc.scalar.copy(
+                out=grouped[:].bitcast(F32).rearrange("p (n u) -> p n u", u=2),
+                in_=bank[:].rearrange("p u n -> p n u"),
+            )
+            codes = const.tile([P, 256], U32, name=label + "_codes", align_bytes=64)
+            scales = const.tile([P, 256], U8, name=label + "_scales", align_bytes=64)
+            nc.vector.quantize_mx(out=codes[:].bitcast(FP8X4), scales=scales[:], in_=grouped[:])
+            return codes, scales
+
+        def passes(bank, wc, ws, codes, scales, cols):
+            for a in range(2):
+                half = slice(a * P, (a + 1) * P)
+                nc.tensor.matmul_mx(
+                    out=bank[:, a, :],
+                    lhsT=wc[:, half].bitcast(FP8X4),
+                    lhsT_scale=ws[:, half],
+                    rhs=codes[:, cols].bitcast(FP8X4),
+                    rhs_scale=scales[:, cols],
+                    start=True,
+                    stop=True,
+                )
+
+        w0_rows = load_weight(w0, "w0")
+        load(0)
+        w1_rows = load_weight(w1, "w1")
+        for i in range(1, RAW_BUFS):
+            load(i)
+        w0c, w0s = prepare_weight(w0_rows, "w0")
+        w1c, w1s = prepare_weight(w1_rows, "w1")
+
+        for i in range(n):
+            b0, nb = spans[i]
+            grp = work.tile([P, nb * 2 * D], BF16, name="grp%d" % i, tag="grp", align_bytes=64)
+            nc.vector.tensor_copy(
+                out=grp[:].bitcast(F32).rearrange("p (b q u) -> p b q u", b=nb, u=2),
+                in_=raw[i][:].bitcast(F32).rearrange("p (b u q) -> p b q u", b=nb, u=2),
+            )
+            if i + RAW_BUFS < n:
+                load(i + RAW_BUFS)
+            xc = work.tile([P, nb * Q1], U32, name="xc%d" % i, tag="xc", align_bytes=64)
+            xs = work.tile([P, nb * Q1], U8, name="xs%d" % i, tag="xs", align_bytes=64)
+            nc.vector.quantize_mx(out=xc[:].bitcast(FP8X4), scales=xs[:], in_=grp[:])
+
+            hg = work.tile([P, nb * 2 * Q1], BF16, name="hg%d" % i, tag="hg", align_bytes=64)
+            for j in range(2 * nb):
+                bank = psum1.tile([P, 2, 256], F32, name="l1_%d_%d" % (i, j), tag="ps1")
+                passes(bank, w0c, w0s, xc, xs, slice(j * 256, (j + 1) * 256))
+                nc.scalar.activation(
+                    out=hg[:, j * 512 : (j + 1) * 512].rearrange("p (r a k) -> p r a k", a=2, k=2),
+                    in_=bank[:].rearrange("p a (r k) -> p r a k", k=2),
+                    func=RELU,
+                    scale=SCALE,
+                )
+            hc = work.tile([P, nb * Q2], U32, name="hc%d" % i, tag="hc", align_bytes=64)
+            hs = work.tile([P, nb * Q2], U8, name="hs%d" % i, tag="hs", align_bytes=64)
+            nc.vector.quantize_mx(out=hc[:].bitcast(FP8X4), scales=hs[:], in_=hg[:])
+
+            for j in range(nb):
+                b = b0 + j
+                bank = psum2.tile([P, 2, 256], F32, name="l2_%d" % b, tag="ps2")
+                passes(bank, w1c, w1s, hc, hs, slice(j * 256, (j + 1) * 256))
+                if b % VECTOR_EXIT_EVERY == VECTOR_EXIT_EVERY - 1:
+                    nc.vector.tensor_scalar(
+                        out=out_all[:, b, :],
+                        in0=bank[:].rearrange("p a r -> p (a r)"),
+                        scalar1=SCALE,
+                        scalar2=0.0,
+                        op0=MULT,
+                        op1=MAX,
+                    )
+                else:
+                    nc.scalar.activation(
+                        out=out_all[:, b, :],
+                        in_=bank[:].rearrange("p a r -> p (a r)"),
+                        func=RELU,
+                        scale=SCALE,
+                    )
+            nc.sync.dma_start(
+                out=out[b0 : b0 + nb].rearrange("b (p a) r -> p b (a r)", a=2),
+                in_=out_all[:, b0 : b0 + nb, :],
+            )

@@ -21,9 +21,11 @@ SCALE = 1.0 / 16.0
 
 FLOPS = 2 * BS * Q1 * 512 * 256 + 2 * BS * Q2 * 512 * 256
 
-CHUNKS = [1, 1, 1, 1] + [2] * 13 + [1, 1]
+CHUNKS = [1] * 8 + [2] * 11 + [1] * 2
 RAW_BUFS = 10
-VECTOR_EXIT_EVERY = 5
+LEAD = 2
+LAG2 = 2
+TAIL = 5
 
 
 def tile_cnn_pa_kernel(tc, x, w0, w1, out):
@@ -42,14 +44,29 @@ def tile_cnn_pa_kernel(tc, x, w0, w1, out):
         work = ctx.enter_context(tc.tile_pool(name="work", bufs=3))
         psum1 = ctx.enter_context(tc.psum_pool(name="psum1", bufs=4))
         psum2 = ctx.enter_context(tc.psum_pool(name="psum2", bufs=4))
+        ctx.enter_context(tc.manual_schedule())
 
         ident = const.tile([P, P], F32, name="ident")
         make_identity(nc, ident[:])
         out_all = const.tile([P, BS, 2 * Q2], F32, name="out_all")
 
         raw = {}
+        grp = {}
+        xq = {}
+        hg = {}
+        hq = {}
+        bank1 = {}
+        bank2 = {}
+        wq = {}
+        wbank = {}
+        wrows = {}
+
+        def inside(i):
+            return 0 <= i < n
 
         def load(i):
+            if not inside(i):
+                return
             b0, nb = spans[i]
             t = raw_pool.tile([P, nb * 2 * D], BF16, name="raw%d" % i, tag="raw")
             nc.sync.dma_start(
@@ -61,25 +78,54 @@ def tile_cnn_pa_kernel(tc, x, w0, w1, out):
         def load_weight(w, label):
             rows = const.tile([P, 1024], BF16, name=label + "_rows")
             nc.sync.dma_start(out=rows[:], in_=w.rearrange("(p a) c k -> p (a c k)", a=2))
-            return rows
+            wrows[label] = rows
 
-        def prepare_weight(rows, label):
-            words = rows[:].bitcast(F32).rearrange("p (a c u) -> p a c u", a=2, u=2)
+        def transpose_weight(label):
+            words = wrows[label][:].bitcast(F32).rearrange("p (a c u) -> p a c u", a=2, u=2)
             bank = psum2.tile([P, 2, 256], F32, name=label + "_bank", tag="ps2")
             for u in range(2):
                 for a in range(2):
                     nc.tensor.transpose(bank[:, u, a * P : (a + 1) * P], words[:, a, :, u], ident[:])
+            wbank[label] = bank
+
+        def copy_weight(label):
             grouped = const.tile([P, 1024], BF16, name=label + "_grouped", align_bytes=64)
             nc.scalar.copy(
                 out=grouped[:].bitcast(F32).rearrange("p (n u) -> p n u", u=2),
-                in_=bank[:].rearrange("p u n -> p n u"),
+                in_=wbank[label][:].rearrange("p u n -> p n u"),
             )
+            wbank[label] = grouped
+
+        def quantise_weight(label):
             codes = const.tile([P, 256], U32, name=label + "_codes", align_bytes=64)
             scales = const.tile([P, 256], U8, name=label + "_scales", align_bytes=64)
-            nc.vector.quantize_mx(out=codes[:].bitcast(FP8X4), scales=scales[:], in_=grouped[:])
-            return codes, scales
+            nc.vector.quantize_mx(out=codes[:].bitcast(FP8X4), scales=scales[:], in_=wbank[label][:])
+            wq[label] = (codes, scales)
 
-        def passes(bank, wc, ws, codes, scales, cols):
+        def regroup(i):
+            if not inside(i):
+                return
+            nb = spans[i][1]
+            g = work.tile([P, nb * 2 * D], BF16, name="grp%d" % i, tag="grp", align_bytes=64)
+            nc.vector.tensor_copy(
+                out=g[:].bitcast(F32).rearrange("p (b q u) -> p b q u", b=nb, u=2),
+                in_=raw[i][:].bitcast(F32).rearrange("p (b u q) -> p b q u", b=nb, u=2),
+            )
+            grp[i] = g
+
+        def quantise_x(i):
+            if not inside(i):
+                return
+            nb = spans[i][1]
+            codes = work.tile([P, nb * Q1], U32, name="xc%d" % i, tag="xc", align_bytes=64)
+            scales = work.tile([P, nb * Q1], U8, name="xs%d" % i, tag="xs", align_bytes=64)
+            nc.vector.quantize_mx(out=codes[:].bitcast(FP8X4), scales=scales[:], in_=grp[i][:])
+            xq[i] = (codes, scales)
+
+        def passes(bank, label, operand, j):
+            wc, ws = wq[label]
+            codes, scales = operand
+            cols = slice(j * 256, (j + 1) * 256)
             for a in range(2):
                 half = slice(a * P, (a + 1) * P)
                 nc.tensor.matmul_mx(
@@ -92,62 +138,92 @@ def tile_cnn_pa_kernel(tc, x, w0, w1, out):
                     stop=True,
                 )
 
-        w0_rows = load_weight(w0, "w0")
-        load(0)
-        w1_rows = load_weight(w1, "w1")
-        for i in range(1, RAW_BUFS):
-            load(i)
-        w0c, w0s = prepare_weight(w0_rows, "w0")
-        w1c, w1s = prepare_weight(w1_rows, "w1")
+        def relu_out(on_vector, dst, src):
+            if on_vector:
+                nc.vector.tensor_scalar(out=dst, in0=src, scalar1=SCALE, scalar2=0.0, op0=MULT, op1=MAX)
+            else:
+                nc.scalar.activation(out=dst, in_=src, func=RELU, scale=SCALE)
 
-        for i in range(n):
-            b0, nb = spans[i]
-            grp = work.tile([P, nb * 2 * D], BF16, name="grp%d" % i, tag="grp", align_bytes=64)
-            nc.vector.tensor_copy(
-                out=grp[:].bitcast(F32).rearrange("p (b q u) -> p b q u", b=nb, u=2),
-                in_=raw[i][:].bitcast(F32).rearrange("p (b u q) -> p b q u", b=nb, u=2),
+        def layer1_passes(i, j):
+            bank = psum1.tile([P, 2, 256], F32, name="l1_%d_%d" % (i, j), tag="ps1")
+            passes(bank, "w0", xq[i], j)
+            bank1[(i, j)] = bank
+
+        def layer1_exit(i, j):
+            if j == 0:
+                nb = spans[i][1]
+                hg[i] = work.tile([P, nb * 2 * Q1], BF16, name="hg%d" % i, tag="hg", align_bytes=64)
+            relu_out(
+                i >= n - TAIL and j == 0,
+                hg[i][:, j * 512 : (j + 1) * 512].rearrange("p (r a k) -> p r a k", a=2, k=2),
+                bank1[(i, j)][:].rearrange("p a (r k) -> p r a k", k=2),
             )
-            if i + RAW_BUFS < n:
-                load(i + RAW_BUFS)
-            xc = work.tile([P, nb * Q1], U32, name="xc%d" % i, tag="xc", align_bytes=64)
-            xs = work.tile([P, nb * Q1], U8, name="xs%d" % i, tag="xs", align_bytes=64)
-            nc.vector.quantize_mx(out=xc[:].bitcast(FP8X4), scales=xs[:], in_=grp[:])
 
-            hg = work.tile([P, nb * 2 * Q1], BF16, name="hg%d" % i, tag="hg", align_bytes=64)
-            for j in range(2 * nb):
-                bank = psum1.tile([P, 2, 256], F32, name="l1_%d_%d" % (i, j), tag="ps1")
-                passes(bank, w0c, w0s, xc, xs, slice(j * 256, (j + 1) * 256))
-                nc.scalar.activation(
-                    out=hg[:, j * 512 : (j + 1) * 512].rearrange("p (r a k) -> p r a k", a=2, k=2),
-                    in_=bank[:].rearrange("p a (r k) -> p r a k", k=2),
-                    func=RELU,
-                    scale=SCALE,
-                )
-            hc = work.tile([P, nb * Q2], U32, name="hc%d" % i, tag="hc", align_bytes=64)
-            hs = work.tile([P, nb * Q2], U8, name="hs%d" % i, tag="hs", align_bytes=64)
-            nc.vector.quantize_mx(out=hc[:].bitcast(FP8X4), scales=hs[:], in_=hg[:])
+        def quantise_h(i):
+            if not inside(i):
+                return
+            nb = spans[i][1]
+            codes = work.tile([P, nb * Q2], U32, name="hc%d" % i, tag="hc", align_bytes=64)
+            scales = work.tile([P, nb * Q2], U8, name="hs%d" % i, tag="hs", align_bytes=64)
+            nc.vector.quantize_mx(out=codes[:].bitcast(FP8X4), scales=scales[:], in_=hg[i][:])
+            hq[i] = (codes, scales)
 
+        def layer2_passes(i):
+            if not inside(i):
+                return
+            b0, nb = spans[i]
             for j in range(nb):
-                b = b0 + j
-                bank = psum2.tile([P, 2, 256], F32, name="l2_%d" % b, tag="ps2")
-                passes(bank, w1c, w1s, hc, hs, slice(j * 256, (j + 1) * 256))
-                if b % VECTOR_EXIT_EVERY == VECTOR_EXIT_EVERY - 1:
-                    nc.vector.tensor_scalar(
-                        out=out_all[:, b, :],
-                        in0=bank[:].rearrange("p a r -> p (a r)"),
-                        scalar1=SCALE,
-                        scalar2=0.0,
-                        op0=MULT,
-                        op1=MAX,
-                    )
-                else:
-                    nc.scalar.activation(
-                        out=out_all[:, b, :],
-                        in_=bank[:].rearrange("p a r -> p (a r)"),
-                        func=RELU,
-                        scale=SCALE,
-                    )
+                bank = psum2.tile([P, 2, 256], F32, name="l2_%d" % (b0 + j), tag="ps2")
+                passes(bank, "w1", hq[i], j)
+                bank2[b0 + j] = bank
+
+        def layer2_exit_and_store(i):
+            if not inside(i):
+                return
+            b0, nb = spans[i]
+            for b in range(b0, b0 + nb):
+                relu_out(False, out_all[:, b, :], bank2[b][:].rearrange("p a r -> p (a r)"))
             nc.sync.dma_start(
                 out=out[b0 : b0 + nb].rearrange("b (p a) r -> p b (a r)", a=2),
                 in_=out_all[:, b0 : b0 + nb, :],
             )
+
+        load_weight(w0, "w0")
+        load(0)
+        load(1)
+        load_weight(w1, "w1")
+        for i in range(2, RAW_BUFS):
+            load(i)
+        transpose_weight("w0")
+        copy_weight("w0")
+        regroup(0)
+        load(RAW_BUFS)
+        quantise_x(0)
+        quantise_weight("w0")
+        for j in range(2 * spans[0][1]):
+            layer1_passes(0, j)
+        for i in range(1, LEAD + 1):
+            regroup(i)
+            load(i + RAW_BUFS)
+            quantise_x(i)
+
+        for s in range(n + LAG2):
+            regroup(s + LEAD + 1)
+            load(s + LEAD + 1 + RAW_BUFS)
+            if s == 1:
+                quantise_weight("w1")
+            quantise_h(s - 1)
+            if s > 0:
+                quantise_x(s + LEAD)
+            exits = 2 * spans[s][1] if inside(s) else 0
+            fills = 2 * spans[s + 1][1] if inside(s + 1) else 0
+            for j in range(max(exits, fills)):
+                if j < exits:
+                    layer1_exit(s, j)
+                if j < fills:
+                    layer1_passes(s + 1, j)
+            if s == 0:
+                transpose_weight("w1")
+                copy_weight("w1")
+            layer2_passes(s - 1)
+            layer2_exit_and_store(s - LAG2)

@@ -15,28 +15,26 @@ MAX = mybir.AluOpType.max
 P = 128
 BS = 32
 D = 1024
-Q1 = 512
 Q2 = 256
+BANK = 256
 SCALE = 1.0 / 16.0
 
-FLOPS = 2 * BS * Q1 * 512 * 256 + 2 * BS * Q2 * 512 * 256
+FLOPS = 2 * BS * 512 * 512 * 256 + 2 * BS * Q2 * 512 * 256
 
-CHUNKS = [1] * 8 + [2] * 11 + [1] * 2
-RAW_BUFS = 10
+RAW_BUFS = 16
 LEAD = 2
 LAG2 = 2
-TAIL = 5
+V_FROM = 8
+V_EVERY = 6
+V_TAIL = 2
 
 
 def tile_cnn_pa_kernel(tc, x, w0, w1, out):
     nc = tc.nc
-    spans = []
-    first = 0
-    for nb in CHUNKS:
-        spans.append((first, nb))
-        first += nb
-    assert first == BS
-    n = len(spans)
+    pieces = [(0, 0, 1), (0, 1, 1)] + [(b, 0, 2) for b in range(1, BS)]
+    of_batch = {}
+    for t, (b, j0, nj) in enumerate(pieces):
+        of_batch[b] = of_batch.get(b, []) + [t]
 
     with ExitStack() as ctx:
         const = ctx.enter_context(tc.tile_pool(name="const", bufs=1))
@@ -58,74 +56,85 @@ def tile_cnn_pa_kernel(tc, x, w0, w1, out):
         bank1 = {}
         bank2 = {}
         wq = {}
-        wbank = {}
-        wrows = {}
+        wstage = {}
+        loaded = [0]
 
-        def inside(i):
-            return 0 <= i < n
+        def inside(b):
+            return 0 <= b < BS
 
-        def load(i):
-            if not inside(i):
+        def load_next():
+            t = loaded[0]
+            if t >= len(pieces):
                 return
-            b0, nb = spans[i]
-            t = raw_pool.tile([P, nb * 2 * D], BF16, name="raw%d" % i, tag="raw")
+            loaded[0] = t + 1
+            b, j0, nj = pieces[t]
+            width = nj * D // 2
+            r = raw_pool.tile([P, 2 * width], BF16, name="raw%d" % t, tag="raw")
             nc.sync.dma_start(
-                out=t[:].rearrange("p (b e) -> p b e", b=nb),
-                in_=x[b0 : b0 + nb].rearrange("b (p u) d -> p b (u d)", u=2),
+                out=r[:].rearrange("p (u d) -> p u d", u=2),
+                in_=x[b].rearrange("(p u) d -> p u d", u=2)[:, :, j0 * (D // 2) : j0 * (D // 2) + width],
             )
-            raw[i] = t
+            raw[t] = r
 
         def load_weight(w, label):
             rows = const.tile([P, 1024], BF16, name=label + "_rows")
             nc.sync.dma_start(out=rows[:], in_=w.rearrange("(p a) c k -> p (a c k)", a=2))
-            wrows[label] = rows
+            wstage[label] = rows
 
         def transpose_weight(label):
-            words = wrows[label][:].bitcast(F32).rearrange("p (a c u) -> p a c u", a=2, u=2)
+            words = wstage[label][:].bitcast(F32).rearrange("p (a c u) -> p a c u", a=2, u=2)
             bank = psum2.tile([P, 2, 256], F32, name=label + "_bank", tag="ps2")
             for u in range(2):
                 for a in range(2):
                     nc.tensor.transpose(bank[:, u, a * P : (a + 1) * P], words[:, a, :, u], ident[:])
-            wbank[label] = bank
+            wstage[label] = bank
 
         def copy_weight(label):
             grouped = const.tile([P, 1024], BF16, name=label + "_grouped", align_bytes=64)
             nc.scalar.copy(
                 out=grouped[:].bitcast(F32).rearrange("p (n u) -> p n u", u=2),
-                in_=wbank[label][:].rearrange("p u n -> p n u"),
+                in_=wstage[label][:].rearrange("p u n -> p n u"),
             )
-            wbank[label] = grouped
+            wstage[label] = grouped
 
         def quantise_weight(label):
             codes = const.tile([P, 256], U32, name=label + "_codes", align_bytes=64)
             scales = const.tile([P, 256], U8, name=label + "_scales", align_bytes=64)
-            nc.vector.quantize_mx(out=codes[:].bitcast(FP8X4), scales=scales[:], in_=wbank[label][:])
+            nc.vector.quantize_mx(out=codes[:].bitcast(FP8X4), scales=scales[:], in_=wstage[label][:])
             wq[label] = (codes, scales)
 
-        def regroup(i):
-            if not inside(i):
-                return
-            nb = spans[i][1]
-            g = work.tile([P, nb * 2 * D], BF16, name="grp%d" % i, tag="grp", align_bytes=64)
+        def regroup_piece(t):
+            nj = pieces[t][2]
+            g = work.tile([P, nj * 4 * BANK], BF16, name="grp%d" % t, tag="grp", align_bytes=64)
             nc.vector.tensor_copy(
-                out=g[:].bitcast(F32).rearrange("p (b q u) -> p b q u", b=nb, u=2),
-                in_=raw[i][:].bitcast(F32).rearrange("p (b u q) -> p b q u", b=nb, u=2),
+                out=g[:].bitcast(F32).rearrange("p (q u) -> p q u", u=2),
+                in_=raw[t][:].bitcast(F32).rearrange("p (u q) -> p q u", u=2),
             )
-            grp[i] = g
+            grp[t] = g
+            load_next()
 
-        def quantise_x(i):
-            if not inside(i):
-                return
-            nb = spans[i][1]
-            codes = work.tile([P, nb * Q1], U32, name="xc%d" % i, tag="xc", align_bytes=64)
-            scales = work.tile([P, nb * Q1], U8, name="xs%d" % i, tag="xs", align_bytes=64)
-            nc.vector.quantize_mx(out=codes[:].bitcast(FP8X4), scales=scales[:], in_=grp[i][:])
-            xq[i] = (codes, scales)
+        def quantise_piece(t):
+            nj = pieces[t][2]
+            codes = work.tile([P, nj * BANK], U32, name="xc%d" % t, tag="xc", align_bytes=64)
+            scales = work.tile([P, nj * BANK], U8, name="xs%d" % t, tag="xs", align_bytes=64)
+            nc.vector.quantize_mx(out=codes[:].bitcast(FP8X4), scales=scales[:], in_=grp[t][:])
+            for j in range(nj):
+                xq[(pieces[t][0], pieces[t][1] + j)] = (codes, scales, j)
 
-        def passes(bank, label, operand, j):
+        def regroup(b):
+            if inside(b):
+                for t in of_batch[b]:
+                    regroup_piece(t)
+
+        def quantise_x(b):
+            if inside(b):
+                for t in of_batch[b]:
+                    quantise_piece(t)
+
+        def passes(bank, label, operand):
             wc, ws = wq[label]
-            codes, scales = operand
-            cols = slice(j * 256, (j + 1) * 256)
+            codes, scales, j = operand
+            cols = slice(j * BANK, (j + 1) * BANK)
             for a in range(2):
                 half = slice(a * P, (a + 1) * P)
                 nc.tensor.matmul_mx(
@@ -144,86 +153,80 @@ def tile_cnn_pa_kernel(tc, x, w0, w1, out):
             else:
                 nc.scalar.activation(out=dst, in_=src, func=RELU, scale=SCALE)
 
-        def layer1_passes(i, j):
-            bank = psum1.tile([P, 2, 256], F32, name="l1_%d_%d" % (i, j), tag="ps1")
-            passes(bank, "w0", xq[i], j)
-            bank1[(i, j)] = bank
+        def layer1_passes(b, j):
+            if not inside(b):
+                return
+            bank = psum1.tile([P, 2, BANK], F32, name="l1_%d_%d" % (b, j), tag="ps1")
+            passes(bank, "w0", xq[(b, j)])
+            bank1[(b, j)] = bank
 
-        def layer1_exit(i, j):
+        def layer1_exit(b, j):
+            if not inside(b):
+                return
             if j == 0:
-                nb = spans[i][1]
-                hg[i] = work.tile([P, nb * 2 * Q1], BF16, name="hg%d" % i, tag="hg", align_bytes=64)
+                hg[b] = work.tile([P, 4 * Q2], BF16, name="hg%d" % b, tag="hg", align_bytes=64)
             relu_out(
-                i >= n - TAIL and j == 0,
-                hg[i][:, j * 512 : (j + 1) * 512].rearrange("p (r a k) -> p r a k", a=2, k=2),
-                bank1[(i, j)][:].rearrange("p a (r k) -> p r a k", k=2),
+                b >= BS - V_TAIL and j == 0,
+                hg[b][:, j * 512 : (j + 1) * 512].rearrange("p (r a k) -> p r a k", a=2, k=2),
+                bank1[(b, j)][:].rearrange("p a (r k) -> p r a k", k=2),
             )
 
-        def quantise_h(i):
-            if not inside(i):
+        def quantise_h(b):
+            if not inside(b):
                 return
-            nb = spans[i][1]
-            codes = work.tile([P, nb * Q2], U32, name="hc%d" % i, tag="hc", align_bytes=64)
-            scales = work.tile([P, nb * Q2], U8, name="hs%d" % i, tag="hs", align_bytes=64)
-            nc.vector.quantize_mx(out=codes[:].bitcast(FP8X4), scales=scales[:], in_=hg[i][:])
-            hq[i] = (codes, scales)
+            codes = work.tile([P, Q2], U32, name="hc%d" % b, tag="hc", align_bytes=64)
+            scales = work.tile([P, Q2], U8, name="hs%d" % b, tag="hs", align_bytes=64)
+            nc.vector.quantize_mx(out=codes[:].bitcast(FP8X4), scales=scales[:], in_=hg[b][:])
+            hq[b] = (codes, scales, 0)
 
-        def layer2_passes(i):
-            if not inside(i):
+        def layer2_passes(b):
+            if not inside(b):
                 return
-            b0, nb = spans[i]
-            for j in range(nb):
-                bank = psum2.tile([P, 2, 256], F32, name="l2_%d" % (b0 + j), tag="ps2")
-                passes(bank, "w1", hq[i], j)
-                bank2[b0 + j] = bank
+            bank = psum2.tile([P, 2, Q2], F32, name="l2_%d" % b, tag="ps2")
+            passes(bank, "w1", hq[b])
+            bank2[b] = bank
 
-        def layer2_exit_and_store(i):
-            if not inside(i):
-                return
-            b0, nb = spans[i]
-            for b in range(b0, b0 + nb):
-                relu_out(False, out_all[:, b, :], bank2[b][:].rearrange("p a r -> p (a r)"))
-            nc.sync.dma_start(
-                out=out[b0 : b0 + nb].rearrange("b (p a) r -> p b (a r)", a=2),
-                in_=out_all[:, b0 : b0 + nb, :],
-            )
+        def vector_takes(b):
+            return b >= V_FROM and b % V_EVERY == 0
 
+        def layer2_exit(b, on_vector):
+            if inside(b) and vector_takes(b) == on_vector:
+                relu_out(on_vector, out_all[:, b, :], bank2[b][:].rearrange("p a r -> p (a r)"))
+
+        def store(b):
+            if inside(b):
+                nc.sync.dma_start(out=out[b].rearrange("(p a) r -> p (a r)", a=2), in_=out_all[:, b, :])
+
+        load_next()
         load_weight(w0, "w0")
-        load(0)
-        load(1)
         load_weight(w1, "w1")
-        for i in range(2, RAW_BUFS):
-            load(i)
+        for t in range(1, RAW_BUFS):
+            load_next()
         transpose_weight("w0")
+        transpose_weight("w1")
         copy_weight("w0")
-        regroup(0)
-        load(RAW_BUFS)
-        quantise_x(0)
+        copy_weight("w1")
+        for t in of_batch[0]:
+            regroup_piece(t)
+            quantise_piece(t)
         quantise_weight("w0")
-        for j in range(2 * spans[0][1]):
+        for j in range(2):
             layer1_passes(0, j)
-        for i in range(1, LEAD + 1):
-            regroup(i)
-            load(i + RAW_BUFS)
-            quantise_x(i)
+        for b in range(1, LEAD + 1):
+            regroup(b)
+            quantise_x(b)
 
-        for s in range(n + LAG2):
+        for s in range(BS + LAG2):
             regroup(s + LEAD + 1)
-            load(s + LEAD + 1 + RAW_BUFS)
             if s == 1:
                 quantise_weight("w1")
             quantise_h(s - 1)
+            layer2_exit(s - LAG2, True)
             if s > 0:
                 quantise_x(s + LEAD)
-            exits = 2 * spans[s][1] if inside(s) else 0
-            fills = 2 * spans[s + 1][1] if inside(s + 1) else 0
-            for j in range(max(exits, fills)):
-                if j < exits:
-                    layer1_exit(s, j)
-                if j < fills:
-                    layer1_passes(s + 1, j)
-            if s == 0:
-                transpose_weight("w1")
-                copy_weight("w1")
+            for j in range(2):
+                layer1_exit(s, j)
+                layer1_passes(s + 1, j)
             layer2_passes(s - 1)
-            layer2_exit_and_store(s - LAG2)
+            layer2_exit(s - LAG2, False)
+            store(s - LAG2)

@@ -21,7 +21,9 @@ SCALE = 1.0 / 16.0
 
 FLOPS = 2 * BS * 512 * 512 * 256 + 2 * BS * Q2 * 512 * 256
 
-RAW_BUFS = 16
+RAW_BUFS = 9
+SINGLE_LOADS = 5
+SINGLE_STORES = 2
 LEAD = 2
 LAG2 = 2
 V_FROM = 8
@@ -35,6 +37,8 @@ def tile_cnn_pa_kernel(tc, x, w0, w1, out):
     of_batch = {}
     for t, (b, j0, nj) in enumerate(pieces):
         of_batch[b] = of_batch.get(b, []) + [t]
+    groups = [[t] for t in range(SINGLE_LOADS)] + [[t, t + 1] for t in range(SINGLE_LOADS, len(pieces), 2)]
+    last_of_group = [g[-1] for g in groups]
 
     with ExitStack() as ctx:
         const = ctx.enter_context(tc.tile_pool(name="const", bufs=1))
@@ -63,18 +67,26 @@ def tile_cnn_pa_kernel(tc, x, w0, w1, out):
             return 0 <= b < BS
 
         def load_next():
-            t = loaded[0]
-            if t >= len(pieces):
+            g = loaded[0]
+            if g >= len(groups):
                 return
-            loaded[0] = t + 1
-            b, j0, nj = pieces[t]
+            loaded[0] = g + 1
+            b, j0, nj = pieces[groups[g][0]]
+            nb = len(groups[g])
             width = nj * D // 2
-            r = raw_pool.tile([P, 2 * width], BF16, name="raw%d" % t, tag="raw")
-            nc.sync.dma_start(
-                out=r[:].rearrange("p (u d) -> p u d", u=2),
-                in_=x[b].rearrange("(p u) d -> p u d", u=2)[:, :, j0 * (D // 2) : j0 * (D // 2) + width],
-            )
-            raw[t] = r
+            r = raw_pool.tile([P, nb * 2 * width], BF16, name="raw%d" % g, tag="raw")
+            if nb == 1:
+                nc.sync.dma_start(
+                    out=r[:].rearrange("p (u d) -> p u d", u=2),
+                    in_=x[b].rearrange("(p u) d -> p u d", u=2)[:, :, j0 * (D // 2) : j0 * (D // 2) + width],
+                )
+            else:
+                nc.sync.dma_start(
+                    out=r[:].rearrange("p (b e) -> p b e", b=nb),
+                    in_=x[b : b + nb].rearrange("b (p u) d -> p b (u d)", u=2),
+                )
+            for k, t in enumerate(groups[g]):
+                raw[t] = r[:, k * 2 * width : (k + 1) * 2 * width]
 
         def load_weight(w, label):
             rows = const.tile([P, 1024], BF16, name=label + "_rows")
@@ -108,10 +120,11 @@ def tile_cnn_pa_kernel(tc, x, w0, w1, out):
             g = work.tile([P, nj * 4 * BANK], BF16, name="grp%d" % t, tag="grp", align_bytes=64)
             nc.vector.tensor_copy(
                 out=g[:].bitcast(F32).rearrange("p (q u) -> p q u", u=2),
-                in_=raw[t][:].bitcast(F32).rearrange("p (u q) -> p q u", u=2),
+                in_=raw[t].bitcast(F32).rearrange("p (u q) -> p q u", u=2),
             )
             grp[t] = g
-            load_next()
+            if t in last_of_group:
+                load_next()
 
         def quantise_piece(t):
             nj = pieces[t][2]
@@ -194,8 +207,15 @@ def tile_cnn_pa_kernel(tc, x, w0, w1, out):
                 relu_out(on_vector, out_all[:, b, :], bank2[b][:].rearrange("p a r -> p (a r)"))
 
         def store(b):
-            if inside(b):
+            if not inside(b):
+                return
+            if b >= BS - SINGLE_STORES:
                 nc.sync.dma_start(out=out[b].rearrange("(p a) r -> p (a r)", a=2), in_=out_all[:, b, :])
+            elif b % 2 == 1:
+                nc.sync.dma_start(
+                    out=out[b - 1 : b + 1].rearrange("b (p a) r -> p b (a r)", a=2),
+                    in_=out_all[:, b - 1 : b + 1, :],
+                )
 
         load_next()
         load_weight(w0, "w0")

@@ -21,9 +21,7 @@ SCALE = 1.0 / 16.0
 
 FLOPS = 2 * BS * 512 * 512 * 256 + 2 * BS * Q2 * 512 * 256
 
-RAW_BUFS = 9
-SINGLE_LOADS = 5
-SINGLE_STORES = 2
+RAW_BUFS = 16
 LEAD = 2
 LAG2 = 2
 V_FROM = 8
@@ -37,8 +35,6 @@ def tile_cnn_pa_kernel(tc, x, w0, w1, out):
     of_batch = {}
     for t, (b, j0, nj) in enumerate(pieces):
         of_batch[b] = of_batch.get(b, []) + [t]
-    groups = [[t] for t in range(SINGLE_LOADS)] + [[t, t + 1] for t in range(SINGLE_LOADS, len(pieces), 2)]
-    last_of_group = [g[-1] for g in groups]
 
     with ExitStack() as ctx:
         const = ctx.enter_context(tc.tile_pool(name="const", bufs=1))
@@ -67,26 +63,18 @@ def tile_cnn_pa_kernel(tc, x, w0, w1, out):
             return 0 <= b < BS
 
         def load_next():
-            g = loaded[0]
-            if g >= len(groups):
+            t = loaded[0]
+            if t >= len(pieces):
                 return
-            loaded[0] = g + 1
-            b, j0, nj = pieces[groups[g][0]]
-            nb = len(groups[g])
+            loaded[0] = t + 1
+            b, j0, nj = pieces[t]
             width = nj * D // 2
-            r = raw_pool.tile([P, nb * 2 * width], BF16, name="raw%d" % g, tag="raw")
-            if nb == 1:
-                nc.sync.dma_start(
-                    out=r[:].rearrange("p (u d) -> p u d", u=2),
-                    in_=x[b].rearrange("(p u) d -> p u d", u=2)[:, :, j0 * (D // 2) : j0 * (D // 2) + width],
-                )
-            else:
-                nc.sync.dma_start(
-                    out=r[:].rearrange("p (b e) -> p b e", b=nb),
-                    in_=x[b : b + nb].rearrange("b (p u) d -> p b (u d)", u=2),
-                )
-            for k, t in enumerate(groups[g]):
-                raw[t] = r[:, k * 2 * width : (k + 1) * 2 * width]
+            r = raw_pool.tile([P, 2 * width], BF16, name="raw%d" % t, tag="raw")
+            nc.sync.dma_start(
+                out=r[:].rearrange("p (u d) -> p u d", u=2),
+                in_=x[b].rearrange("(p u) d -> p u d", u=2)[:, :, j0 * (D // 2) : j0 * (D // 2) + width],
+            )
+            raw[t] = r
 
         def load_weight(w, label):
             rows = const.tile([P, 1024], BF16, name=label + "_rows")
@@ -119,12 +107,11 @@ def tile_cnn_pa_kernel(tc, x, w0, w1, out):
             nj = pieces[t][2]
             g = work.tile([P, nj * 4 * BANK], BF16, name="grp%d" % t, tag="grp", align_bytes=64)
             nc.vector.tensor_copy(
-                out=g[:].bitcast(F32).rearrange("p (q u) -> p q u", u=2),
-                in_=raw[t].bitcast(F32).rearrange("p (u q) -> p q u", u=2),
+                out=g[:].bitcast(F32).rearrange("p (c i u) -> p c u i", i=4, u=2),
+                in_=raw[t][:].bitcast(F32).rearrange("p (u c i) -> p c u i", i=4, u=2),
             )
             grp[t] = g
-            if t in last_of_group:
-                load_next()
+            load_next()
 
         def quantise_piece(t):
             nj = pieces[t][2]
@@ -207,15 +194,8 @@ def tile_cnn_pa_kernel(tc, x, w0, w1, out):
                 relu_out(on_vector, out_all[:, b, :], bank2[b][:].rearrange("p a r -> p (a r)"))
 
         def store(b):
-            if not inside(b):
-                return
-            if b >= BS - SINGLE_STORES:
+            if inside(b):
                 nc.sync.dma_start(out=out[b].rearrange("(p a) r -> p (a r)", a=2), in_=out_all[:, b, :])
-            elif b % 2 == 1:
-                nc.sync.dma_start(
-                    out=out[b - 1 : b + 1].rearrange("b (p a) r -> p b (a r)", a=2),
-                    in_=out_all[:, b - 1 : b + 1, :],
-                )
 
         load_next()
         load_weight(w0, "w0")

from contextlib import ExitStack

import concourse.mybir as mybir
from concourse.masks import make_identity

FP8X4 = mybir.dt.float8_e4m3fn_x4
BF16 = mybir.dt.bfloat16
F32 = mybir.dt.float32
U32 = mybir.dt.uint32
U8 = mybir.dt.uint8
RELU = mybir.ActivationFunctionType.Relu
MULT = mybir.AluOpType.mult
MAX = mybir.AluOpType.max

P = 128
BS = 32
D = 1024
Q2 = 256
BANK = 256
SCALE = 1.0 / 16.0

FLOPS = 2 * BS * 512 * 512 * 256 + 2 * BS * Q2 * 512 * 256

RAW_BUFS = 16
LEAD = 2
LAG2 = 2
V_FROM = 8
V_EVERY = 6
V_TAIL = 2


def tile_cnn_pa_kernel(tc, x, w0, w1, out):
    nc = tc.nc
    pieces = [(0, 0, 1), (0, 1, 1)] + [(b, 0, 2) for b in range(1, BS)]
    of_batch = {}
    for t, (b, j0, nj) in enumerate(pieces):
        of_batch[b] = of_batch.get(b, []) + [t]

    with ExitStack() as ctx:
        const = ctx.enter_context(tc.tile_pool(name="const", bufs=1))
        raw_pool = ctx.enter_context(tc.tile_pool(name="rawp", bufs=RAW_BUFS))
        work = ctx.enter_context(tc.tile_pool(name="work", bufs=3))
        psum1 = ctx.enter_context(tc.psum_pool(name="psum1", bufs=4))
        psum2 = ctx.enter_context(tc.psum_pool(name="psum2", bufs=4))
        ctx.enter_context(tc.manual_schedule())

        ident = const.tile([P, P], F32, name="ident")
        make_identity(nc, ident[:])
        out_all = const.tile([P, BS, 2 * Q2], F32, name="out_all")

        raw = {}
        grp = {}
        xq = {}
        hg = {}
        hq = {}
        bank1 = {}
        bank2 = {}
        wq = {}
        wstage = {}
        loaded = [0]

        def inside(b):
            return 0 <= b < BS

        def load_next():
            t = loaded[0]
            if t >= len(pieces):
                return
            loaded[0] = t + 1
            b, j0, nj = pieces[t]
            width = nj * D // 2
            r = raw_pool.tile([P, 2 * width], BF16, name="raw%d" % t, tag="raw")
            nc.sync.dma_start(
                out=r[:].rearrange("p (u d) -> p u d", u=2),
                in_=x[b].rearrange("(p u) d -> p u d", u=2)[:, :, j0 * (D // 2) : j0 * (D // 2) + width],
            )
            raw[t] = r

        def load_weight(w, label):
            rows = const.tile([P, 1024], BF16, name=label + "_rows")
            nc.sync.dma_start(out=rows[:], in_=w.rearrange("(p a) c k -> p (a c k)", a=2))
            wstage[label] = rows

        def transpose_weight(label):
            words = wstage[label][:].bitcast(F32).rearrange("p (a c u) -> p a c u", a=2, u=2)
            bank = psum2.tile([P, 2, 256], F32, name=label + "_bank", tag="ps2")
            for u in range(2):
                for a in range(2):
                    nc.tensor.transpose(bank[:, u, a * P : (a + 1) * P], words[:, a, :, u], ident[:])
            wstage[label] = bank

        def copy_weight(label):
            grouped = const.tile([P, 1024], BF16, name=label + "_grouped", align_bytes=64)
            nc.scalar.copy(
                out=grouped[:].bitcast(F32).rearrange("p (n u) -> p n u", u=2),
                in_=wstage[label][:].rearrange("p u n -> p n u"),
            )
            wstage[label] = grouped

        def quantise_weight(label):
            codes = const.tile([P, 256], U32, name=label + "_codes", align_bytes=64)
            scales = const.tile([P, 256], U8, name=label + "_scales", align_bytes=64)
            nc.vector.quantize_mx(out=codes[:].bitcast(FP8X4), scales=scales[:], in_=wstage[label][:])
            wq[label] = (codes, scales)

        def regroup_piece(t):
            nj = pieces[t][2]
            g = work.tile([P, nj * 4 * BANK], BF16, name="grp%d" % t, tag="grp", align_bytes=64)
            nc.vector.tensor_copy(
                out=g[:].bitcast(F32).rearrange("p (c i u) -> p c u i", i=4, u=2),
                in_=raw[t][:].bitcast(F32).rearrange("p (u c i) -> p c u i", i=4, u=2),
            )
            grp[t] = g
            load_next()

        def quantise_piece(t):
            nj = pieces[t][2]
            codes = work.tile([P, nj * BANK], U32, name="xc%d" % t, tag="xc", align_bytes=64)
            scales = work.tile([P, nj * BANK], U8, name="xs%d" % t, tag="xs", align_bytes=64)
            nc.vector.quantize_mx(out=codes[:].bitcast(FP8X4), scales=scales[:], in_=grp[t][:])
            for j in range(nj):
                xq[(pieces[t][0], pieces[t][1] + j)] = (codes, scales, j)

        def regroup(b):
            if inside(b):
                for t in of_batch[b]:
                    regroup_piece(t)

        def quantise_x(b):
            if inside(b):
                for t in of_batch[b]:
                    quantise_piece(t)

        def passes(bank, label, operand):
            wc, ws = wq[label]
            codes, scales, j = operand
            cols = slice(j * BANK, (j + 1) * BANK)
            for a in range(2):
                half = slice(a * P, (a + 1) * P)
                nc.tensor.matmul_mx(
                    out=bank[:, a, :],
                    lhsT=wc[:, half].bitcast(FP8X4),
                    lhsT_scale=ws[:, half],
                    rhs=codes[:, cols].bitcast(FP8X4),
                    rhs_scale=scales[:, cols],
                    start=True,
                    stop=True,
                )

        def relu_out(on_vector, dst, src):
            if on_vector:
                nc.vector.tensor_scalar(out=dst, in0=src, scalar1=SCALE, scalar2=0.0, op0=MULT, op1=MAX)
            else:
                nc.scalar.activation(out=dst, in_=src, func=RELU, scale=SCALE)

        def layer1_passes(b, j):
            if not inside(b):
                return
            bank = psum1.tile([P, 2, BANK], F32, name="l1_%d_%d" % (b, j), tag="ps1")
            passes(bank, "w0", xq[(b, j)])
            bank1[(b, j)] = bank

        def layer1_exit(b, j):
            if not inside(b):
                return
            if j == 0:
                hg[b] = work.tile([P, 4 * Q2], BF16, name="hg%d" % b, tag="hg", align_bytes=64)
            relu_out(
                b >= BS - V_TAIL and j == 0,
                hg[b][:, j * 512 : (j + 1) * 512].rearrange("p (r a k) -> p r a k", a=2, k=2),
                bank1[(b, j)][:].rearrange("p a (r k) -> p r a k", k=2),
            )

        def quantise_h(b):
            if not inside(b):
                return
            codes = work.tile([P, Q2], U32, name="hc%d" % b, tag="hc", align_bytes=64)
            scales = work.tile([P, Q2], U8, name="hs%d" % b, tag="hs", align_bytes=64)
            nc.vector.quantize_mx(out=codes[:].bitcast(FP8X4), scales=scales[:], in_=hg[b][:])
            hq[b] = (codes, scales, 0)

        def layer2_passes(b):
            if not inside(b):
                return
            bank = psum2.tile([P, 2, Q2], F32, name="l2_%d" % b, tag="ps2")
            passes(bank, "w1", hq[b])
            bank2[b] = bank

        def vector_takes(b):
            return b >= V_FROM and b % V_EVERY == 0

        def layer2_exit(b, on_vector):
            if inside(b) and vector_takes(b) == on_vector:
                relu_out(on_vector, out_all[:, b, :], bank2[b][:].rearrange("p a r -> p (a r)"))

        def store(b):
            if inside(b):
                nc.sync.dma_start(out=out[b].rearrange("(p a) r -> p (a r)", a=2), in_=out_all[:, b, :])

        load_next()
        load_weight(w0, "w0")
        load_weight(w1, "w1")
        for t in range(1, RAW_BUFS):
            load_next()
        transpose_weight("w0")
        transpose_weight("w1")
        copy_weight("w0")
        copy_weight("w1")
        for t in of_batch[0]:
            regroup_piece(t)
            quantise_piece(t)
        quantise_weight("w0")
        for j in range(2):
            layer1_passes(0, j)
        for b in range(1, LEAD + 1):
            regroup(b)
            quantise_x(b)

        for s in range(BS + LAG2):
            regroup(s + LEAD + 1)
            if s == 1:
                quantise_weight("w1")
            quantise_h(s - 1)
            layer2_exit(s - LAG2, True)
            if s > 0:
                quantise_x(s + LEAD)
            for j in range(2):
                layer1_exit(s, j)
                layer1_passes(s + 1, j)
            layer2_passes(s - 1)
            layer2_exit(s - LAG2, False)
            store(s - LAG2)
